import numpy as np
import ml_dtypes


def mxq(x, axis, fmt="e4m3"):
    dtype, down = {"e4m3": (ml_dtypes.float8_e4m3fn, 7), "e5m2": (ml_dtypes.float8_e5m2, 14)}[fmt]
    v = np.moveaxis(np.asarray(x, np.float32).astype(ml_dtypes.bfloat16).astype(np.float64), axis, -1)
    blocks = v.reshape(v.shape[:-1] + (-1, 32))
    amax = np.abs(blocks).max(-1, keepdims=True)
    byte = np.maximum(np.where(amax > 0, np.frexp(amax)[1] - 1 + 127, 0) - down, 1)
    scale = np.exp2(byte - 127.0)
    codes = (blocks / scale).astype(np.float32).astype(dtype).astype(np.float64)
    return np.moveaxis((codes * scale).reshape(v.shape), -1, axis)


WIDE = False


def mx_kscale(k):
    if not WIDE:
        return np.ones(k)
    levels = np.array([10, -10, 5, -5, 0])
    if k % 512:
        return np.exp2(np.random.permutation(np.resize(levels, k // 32))).repeat(32)
    a = np.empty((k // 512, 16))
    for p in range(k // 512):
        a[p, :8] = np.random.permutation(np.resize(levels, 8))
        for g in range(8):
            far = levels[np.abs(levels - a[p, g]) >= 10]
            a[p, g + 8] = far[np.random.randint(len(far))]
    return np.exp2(a.ravel()).repeat(32)


BF16 = ml_dtypes.bfloat16


def bf(x):
    return np.asarray(x, np.float32).astype(BF16)


def f64(x):
    return np.asarray(x).astype(np.float64)


B, D, U = 256, 1024, 1024
KD = 3 * U + D


def sigmoid(v):
    return 1.0 / (1.0 + np.exp(-v))


def setup_inputs():
    s = mx_kscale(KD)

    def gate():
        return bf(np.random.standard_normal((KD, U)) * 1.25 / np.sqrt(KD) / s[:, None])

    def bias():
        return bf(np.random.standard_normal(U) * 0.5)

    return {"x": bf(np.random.standard_normal((B, D)) * s[3 * U:]),
            "left_state": bf(np.random.standard_normal((B, U)) * s[:U]),
            "top_state": bf(np.random.standard_normal((B, U)) * s[U:2 * U]),
            "diagonal_state": bf(np.random.standard_normal((B, U)) * s[2 * U:3 * U]),
            "w_rl": gate(), "b_rl": bias(), "w_rt": gate(), "b_rt": bias(), "w_rd": gate(), "b_rd": bias(),
            "u": bf(np.random.standard_normal((3 * U, U)) * 1.1 / np.sqrt(3 * U) / s[:3 * U, None]),
            "w_i": bf(np.random.standard_normal((D, U)) * 0.65 / np.sqrt(D) / s[3 * U:, None]),
            "b_i": bf(np.random.standard_normal(U) * 0.3)}


def reference(x, left_state, top_state, diagonal_state, w_rl, b_rl, w_rt, b_rt, w_rd, b_rd, u, w_i, b_i):
    states = np.concatenate([f64(left_state), f64(top_state), f64(diagonal_state)], axis=1)
    q = np.concatenate([states, f64(x)], axis=1)
    W = np.concatenate([f64(w_rl), f64(w_rt), f64(w_rd)], axis=1)
    b = np.concatenate([f64(b_rl), f64(b_rt), f64(b_rd)])
    qq = mxq(q, 1, "e4m3")
    reset = sigmoid((qq @ mxq(W, 0, "e4m3")) + b)
    xq = qq[:, 3 * U:]
    return np.tanh((xq @ mxq(f64(w_i), 0, "e4m3")) + f64(b_i)
                   + (mxq(reset * states, 1, "e4m3") @ mxq(f64(u), 0, "e4m3")))

@@ -1,0 +1,269 @@
+from contextlib import ExitStack
+
+import concourse.mybir as mybir
+from concourse.masks import make_identity
+
+F32 = mybir.dt.float32
+BF16 = mybir.dt.bfloat16
+U32 = mybir.dt.uint32
+U8 = mybir.dt.uint8
+FP8X4 = mybir.dt.float8_e4m3fn_x4
+ACT = mybir.ActivationFunctionType
+ALU = mybir.AluOpType
+
+P = 128
+PACK = 4
+K_PASS = P * PACK
+BATCH = 256
+UNITS = 1024
+FLOPS = 2 * BATCH * (4 * UNITS * 3 * UNITS + UNITS * UNITS + 3 * UNITS * UNITS)
+
+RAW_BUFS = 8
+
+
+def v_cols(n):
+    if n in (10, 18, 26):
+        return 944
+    if n in (12, 13, 20, 21, 28, 29):
+        return 200
+    if n == 31:
+        return 432
+    if 2 <= n <= 5:
+        return 560
+    return 520
+
+
+def tile_multidimensinalgrucell_pa_kernel(
+    tc, x, left_state, top_state, diagonal_state,
+    w_rl, b_rl, w_rt, b_rt, w_rd, b_rd, u, w_i, b_i, out,
+):
+    nc = tc.nc
+    chunks = []
+    for gi, w in enumerate((w_rl, w_rt, w_rd)):
+        for c in range(8):
+            chunks.append(("gate", w, c, gi))
+    for c in range(2):
+        chunks.append(("wi", w_i, c, 0))
+    for c in range(6):
+        chunks.append(("u", u, c, 0))
+    n_chunks = len(chunks)
+    q_inputs = (left_state, top_state, diagonal_state, x)
+
+    with ExitStack() as ctx:
+        const = ctx.enter_context(tc.tile_pool(name="const", bufs=1))
+        rawp = ctx.enter_context(tc.tile_pool(name="rawp", bufs=RAW_BUFS))
+        grpp = ctx.enter_context(tc.tile_pool(name="grpp", bufs=4))
+        codep = ctx.enter_context(tc.tile_pool(name="codep", bufs=5))
+        sigp = ctx.enter_context(tc.tile_pool(name="sigp", bufs=2))
+        outp = ctx.enter_context(tc.tile_pool(name="outp", bufs=4))
+        psum = ctx.enter_context(tc.psum_pool(name="psum", bufs=1))
+        ctx.enter_context(tc.manual_schedule())
+
+        raws = {}
+        grps = {}
+        codes = {}
+        scls = {}
+        q_raw = {}
+        qg = {}
+        q_cod = {}
+        q_scl = {}
+        rs_cod = {}
+        rs_scl = {}
+        acc = {}
+        sigs = {}
+        biases = {}
+        xts = {}
+
+        def load(n):
+            w, c = chunks[n][1], chunks[n][2]
+            raw = rawp.tile([P, PACK * UNITS], BF16, name="raw")
+            rows = w[c * K_PASS:(c + 1) * K_PASS, :]
+            nc.sync.dma_start(out=raw[:], in_=rows.rearrange("(p j) n -> p (j n)", j=PACK))
+            raws[n] = raw
+
+        def load_q(i):
+            qr = const.tile([P, 2 * UNITS], BF16, name="q_raw%d" % i)
+            nc.sync.dma_start(
+                out=qr[:].rearrange("p (b k) -> p b k", b=2),
+                in_=q_inputs[i].rearrange("(b p) k -> p b k", p=P),
+            )
+            q_raw[i] = qr
+
+        def regroup(n):
+            grp = grpp.tile([P, PACK * UNITS], BF16, name="grp", align_bytes=64)
+            src = raws[n][:].rearrange("p (j c i) -> p c j i", j=PACK, i=4)
+            if chunks[n][0] == "gate":
+                dst = grp[:].rearrange("p (i c j) -> p c j i", i=4, j=PACK)
+            else:
+                dst = grp[:].rearrange("p (c i j) -> p c j i", i=4, j=PACK)
+            cut = v_cols(n) // 4
+            nc.vector.tensor_copy(out=dst[:, 0:cut], in_=src[:, 0:cut])
+            nc.scalar.copy(out=dst[:, cut:], in_=src[:, cut:])
+            grps[n] = grp
+
+        def quant(n):
+            cod = codep.tile([P, UNITS], U32, name="cod", align_bytes=64)
+            scl = codep.tile([P, UNITS], U8, name="scl", align_bytes=64)
+            for half in range(2):
+                nc.vector.quantize_mx(
+                    out=cod[:, 512 * half:512 * half + 512].bitcast(FP8X4),
+                    scales=scl[:, 512 * half:512 * half + 512],
+                    in_=grps[n][:, 2048 * half:2048 * half + 2048],
+                )
+            codes[n] = cod
+            scls[n] = scl
+
+        def q_transposes(i):
+            for c in (2 * i, 2 * i + 1):
+                words = q_raw[i][:].bitcast(F32).rearrange(
+                    "p (b h w e) -> p b h e w", b=2, h=2, w=P, e=2)
+                xt = psum.tile([P, 2, BATCH], F32, name="xt%d" % c, tag="bank%d" % (4 + c % 4))
+                for e in range(2):
+                    for b in range(2):
+                        nc.tensor.transpose(
+                            xt[:, e, b * P:(b + 1) * P], words[:, b, c % 2, e, :], ident[:])
+                xts[c] = xt
+
+        def q_finish(i):
+            for c in (2 * i, 2 * i + 1):
+                g = const.tile([P, PACK * BATCH], BF16, name="qg%d" % c, align_bytes=64)
+                nc.scalar.copy(
+                    out=g[:].bitcast(F32).rearrange("p (b e) -> p b e", e=2),
+                    in_=xts[c][:].rearrange("p e b -> p b e"),
+                )
+                qg[c] = g
+            for c in (2 * i, 2 * i + 1):
+                qc = const.tile([P, BATCH], U32, name="q_cod%d" % c, align_bytes=64)
+                qs = const.tile([P, BATCH], U8, name="q_scl%d" % c, align_bytes=64)
+                nc.vector.quantize_mx(out=qc[:].bitcast(FP8X4), scales=qs[:], in_=qg[c][:])
+                q_cod[c] = qc
+                q_scl[c] = qs
+
+        def tile0(i):
+            return 2 * P * (i % 4) + P * (i // 4)
+
+        def mm(n):
+            kind, w, c, gi = chunks[n]
+            if kind == "gate":
+                for i in range(8):
+                    if c == 0 and i % 2 == 0:
+                        acc[i // 2] = psum.tile(
+                            [P, 512], F32, name="acc%d_%d" % (gi, i // 2),
+                            tag="bank%d" % (4 * (gi % 2) + i // 2))
+                    nc.tensor.matmul_mx(
+                        out=acc[i // 2][:, (i % 2) * BATCH:(i % 2 + 1) * BATCH],
+                        lhsT=codes[n][:, tile0(i):tile0(i) + P].bitcast(FP8X4),
+                        lhsT_scale=scls[n][:, tile0(i):tile0(i) + P],
+                        rhs=q_cod[c][:].bitcast(FP8X4),
+                        rhs_scale=q_scl[c][:],
+                        start=(c == 0 and i % 2 == 0),
+                        stop=(c == 7 and i % 2 == 1),
+                    )
+            else:
+                first = kind == "wi" and c == 0
+                last = kind == "u" and c == 5
+                for h in range(2):
+                    for b in range(2):
+                        i = 2 * h + b
+                        if first:
+                            acc[i] = psum.tile([P, 512], F32, name="acc2_%d" % i, tag="bank%d" % (4 + i))
+                        if kind == "wi":
+                            a_cod, a_scl = q_cod[6 + c], q_scl[6 + c]
+                        else:
+                            a_cod, a_scl = rs_cod[c], rs_scl[c]
+                        nc.tensor.matmul_mx(
+                            out=acc[i][:],
+                            lhsT=a_cod[:, b * P:(b + 1) * P].bitcast(FP8X4),
+                            lhsT_scale=a_scl[:, b * P:(b + 1) * P],
+                            rhs=codes[n][:, 512 * h:512 * h + 512].bitcast(FP8X4),
+                            rhs_scale=scls[n][:, 512 * h:512 * h + 512],
+                            start=first,
+                            stop=last,
+                        )
+
+        def sigmoids(gi):
+            for g in range(2):
+                sig = sigp.tile([P, PACK * BATCH], F32, name="sig")
+                for t in range(PACK):
+                    i = 4 * g + t
+                    nc.scalar.activation(
+                        out=sig[:, t * BATCH:(t + 1) * BATCH],
+                        in_=acc[i // 2][:, (i % 2) * BATCH:(i % 2 + 1) * BATCH],
+                        func=ACT.Sigmoid,
+                        bias=biases[gi][:, i:i + 1],
+                        scale=1.0,
+                    )
+                sigs[g] = sig
+            if gi == 2:
+                nc.scalar.activation(out=warm2[:, 1:2], in_=sigs[1][:, 0:1], func=ACT.Tanh)
+
+        def products(gi):
+            for g in range(2):
+                rsg = sigp.tile([P, PACK * BATCH], BF16, name="rsg", align_bytes=64)
+                nc.vector.tensor_tensor(
+                    out=rsg[:].rearrange("p (b t) -> p b t", t=PACK),
+                    in0=sigs[g][:].rearrange("p (t b) -> p b t", t=PACK),
+                    in1=qg[2 * gi + g][:].rearrange("p (b t) -> p b t", t=PACK),
+                    op=ALU.mult,
+                )
+                sigs[2 + g] = rsg
+            for g in range(2):
+                cc = 2 * gi + g
+                rc = const.tile([P, BATCH], U32, name="rs_cod%d" % cc, align_bytes=64)
+                rsc = const.tile([P, BATCH], U8, name="rs_scl%d" % cc, align_bytes=64)
+                nc.vector.quantize_mx(out=rc[:].bitcast(FP8X4), scales=rsc[:], in_=sigs[2 + g][:])
+                rs_cod[cc] = rc
+                rs_scl[cc] = rsc
+
+        ident = const.tile([P, P], F32, name="ident")
+        make_identity(nc, ident[:])
+        warm = const.tile([P, 2], F32, name="warm")
+        nc.vector.memset(warm[:], 0.0)
+        for gi, b in enumerate((b_rl, b_rt, b_rd)):
+            bias = const.tile([P, 8], BF16, name="bias%d" % gi)
+            nc.gpsimd.dma_start(
+                out=bias[:].rearrange("p (g t) -> p g t", t=PACK),
+                in_=b.rearrange("(g p t) -> p g t", p=P, t=PACK))
+            biases[gi] = bias
+        warm2 = const.tile([P, 2], F32, name="warm2")
+        nc.scalar.activation(out=warm2[:, 0:1], in_=warm[:, 0:1], func=ACT.Sigmoid)
+
+        load(0)
+        for i in range(4):
+            load(i + 1)
+            load_q(i)
+        for n in range(5, RAW_BUFS):
+            load(n)
+
+        bias_bc = const.tile([P, UNITS], BF16, name="bias_bc")
+
+        for n in range(n_chunks + 1):
+            if n < n_chunks:
+                regroup(n)
+            if n in (10, 18, 26):
+                sigmoids((n - 10) // 8)
+            if 1 <= n <= 4:
+                q_transposes(n - 1)
+            if n + RAW_BUFS < n_chunks:
+                load(n + RAW_BUFS)
+            if n == 24:
+                nc.sync.dma_start(out=bias_bc[:], in_=b_i.partition_broadcast(P))
+            if n >= 1:
+                quant(n - 1)
+            if 2 <= n <= 5:
+                q_finish(n - 2)
+            if n >= 2:
+                mm(n - 2)
+            if n in (12, 20, 28):
+                products((n - 12) // 8)
+        mm(n_chunks - 1)
+
+        for h in range(2):
+            for b in range(2):
+                i = 2 * h + b
+                pre = outp.tile([P, 512], F32, name="pre")
+                nc.vector.tensor_tensor(
+                    out=pre[:], in0=acc[i][:], in1=bias_bc[:, 512 * h:512 * h + 512], op=ALU.add)
+                res = outp.tile([P, 512], F32, name="res")
+                nc.scalar.activation(out=res[:], in_=pre[:], func=ACT.Tanh)
+                nc.sync.dma_start(out=out[b * P:(b + 1) * P, 512 * h:512 * h + 512], in_=res[:])

@@ -21,16 +21,25 @@ FLOPS = 2 * BATCH * (4 * UNITS * 3 * UNITS + UNITS * UNITS + 3 * UNITS * UNITS)
 RAW_BUFS = 8
 
 
+T_COLS = 256
+
+
+def carried(n):
+    return n < 2 or (n >= 6 and n % 8 != 2)
+
+
 def v_cols(n):
     if n in (10, 18, 26):
-        return 944
-    if n in (12, 13, 20, 21, 28, 29):
+        return 800
+    if n in (12, 20, 28):
+        return 104
+    if n in (13, 21, 29):
         return 200
     if n == 31:
-        return 432
+        return 384
     if 2 <= n <= 5:
         return 560
-    return 520
+    return 416
 
 
 def tile_multidimensinalgrucell_pa_kernel(
@@ -72,6 +81,7 @@ def tile_multidimensinalgrucell_pa_kernel(
         acc = {}
         sigs = {}
         biases = {}
+        pts = {}
         xts = {}
 
         def load(n):
@@ -97,9 +107,43 @@ def tile_multidimensinalgrucell_pa_kernel(
             else:
                 dst = grp[:].rearrange("p (c i j) -> p c j i", i=4, j=PACK)
             cut = v_cols(n) // 4
+            end = (UNITS - T_COLS) // 4 if carried(n) else UNITS // 4
             nc.vector.tensor_copy(out=dst[:, 0:cut], in_=src[:, 0:cut])
-            nc.scalar.copy(out=dst[:, cut:], in_=src[:, cut:])
+            nc.scalar.copy(out=dst[:, cut:end], in_=src[:, cut:end])
+            if carried(n):
+                if chunks[n][0] == "gate":
+                    laid = grp[:].rearrange("p (i c j) -> p i c j", i=4, j=PACK)[:, :, end:, :]
+                    nc.scalar.copy(
+                        out=laid.rearrange("p i c j -> p i (c j)"),
+                        in_=pts[n][:].rearrange("p (i y) -> p i y", i=4))
+                else:
+                    nc.scalar.copy(out=grp[:, 4 * PACK * end:], in_=pts[n][:])
             grps[n] = grp
+
+        def carry(n):
+            if n >= n_chunks or not carried(n):
+                return
+            gi, r = n // 8, n % 8
+            bank = 4 * (gi % 2) + 2 + r if r < 2 else 4 * ((gi + 1) % 2) + r % 2
+            pt = psum.tile([P, PACK * T_COLS], BF16, name="pt%d" % n, tag="bank%d" % bank)
+            for h in range(2):
+                half = pt[:, 512 * h:512 * h + 512]
+                if chunks[n][0] == "gate":
+                    end = (UNITS - T_COLS) // 4
+                    nc.tensor.matmul(
+                        out=half.rearrange("p (i c j) -> p i c j", i=2, j=PACK),
+                        lhsT=ident_bf[:],
+                        rhs=raws[n][:].rearrange("p (j c i) -> p i c j", j=PACK, i=4)[
+                            :, 2 * h:2 * h + 2, end:, :],
+                        start=True, stop=True)
+                else:
+                    c0 = UNITS - T_COLS + P * h
+                    nc.tensor.matmul(
+                        out=half.rearrange("p (c j) -> p c j", j=PACK),
+                        lhsT=ident_bf[:],
+                        rhs=raws[n][:].rearrange("p (j c) -> p c j", j=PACK)[:, c0:c0 + P, :],
+                        start=True, stop=True)
+            pts[n] = pt
 
         def quant(n):
             cod = codep.tile([P, UNITS], U32, name="cod", align_bytes=64)
@@ -217,6 +261,8 @@ def tile_multidimensinalgrucell_pa_kernel(
 
         ident = const.tile([P, P], F32, name="ident")
         make_identity(nc, ident[:])
+        ident_bf = const.tile([P, P], BF16, name="ident_bf")
+        make_identity(nc, ident_bf[:])
         warm = const.tile([P, 2], F32, name="warm")
         nc.vector.memset(warm[:], 0.0)
         for gi, b in enumerate((b_rl, b_rt, b_rd)):
@@ -237,6 +283,7 @@ def tile_multidimensinalgrucell_pa_kernel(
 
         bias_bc = const.tile([P, UNITS], BF16, name="bias_bc")
 
+        carry(0)
         for n in range(n_chunks + 1):
             if n < n_chunks:
                 regroup(n)
@@ -254,6 +301,7 @@ def tile_multidimensinalgrucell_pa_kernel(
                 q_finish(n - 2)
             if n >= 2:
                 mm(n - 2)
+            carry(n + 1)
             if n in (12, 20, 28):
                 products((n - 12) // 8)
         mm(n_chunks - 1)

@@ -126,23 +126,16 @@ def tile_multidimensinalgrucell_pa_kernel(
             gi, r = n // 8, n % 8
             bank = 4 * (gi % 2) + 2 + r if r < 2 else 4 * ((gi + 1) % 2) + r % 2
             pt = psum.tile([P, PACK * T_COLS], BF16, name="pt%d" % n, tag="bank%d" % bank)
+            src = raws[n][:].rearrange("p (j c i) -> p c j i", j=PACK, i=4)
+            if chunks[n][0] == "gate":
+                dst = pt[:].rearrange("p (i c j) -> p c j i", i=4, j=PACK)
+            else:
+                dst = pt[:].rearrange("p (c i j) -> p c j i", i=4, j=PACK)
+            c0 = (UNITS - T_COLS) // 4
             for h in range(2):
-                half = pt[:, 512 * h:512 * h + 512]
-                if chunks[n][0] == "gate":
-                    end = (UNITS - T_COLS) // 4
-                    nc.tensor.matmul(
-                        out=half.rearrange("p (i c j) -> p i c j", i=2, j=PACK),
-                        lhsT=ident_bf[:],
-                        rhs=raws[n][:].rearrange("p (j c i) -> p i c j", j=PACK, i=4)[
-                            :, 2 * h:2 * h + 2, end:, :],
-                        start=True, stop=True)
-                else:
-                    c0 = UNITS - T_COLS + P * h
-                    nc.tensor.matmul(
-                        out=half.rearrange("p (c j) -> p c j", j=PACK),
-                        lhsT=ident_bf[:],
-                        rhs=raws[n][:].rearrange("p (j c) -> p c j", j=PACK)[:, c0:c0 + P, :],
-                        start=True, stop=True)
+                nc.tensor.matmul(
+                    out=dst[:, 32 * h:32 * h + 32], lhsT=ident_bf[:],
+                    rhs=src[:, c0 + 32 * h:c0 + 32 * h + 32], start=True, stop=True)
             pts[n] = pt
 
         def quant(n):

@@ -126,16 +126,16 @@ def tile_multidimensinalgrucell_pa_kernel(
             gi, r = n // 8, n % 8
             bank = 4 * (gi % 2) + 2 + r if r < 2 else 4 * ((gi + 1) % 2) + r % 2
             pt = psum.tile([P, PACK * T_COLS], BF16, name="pt%d" % n, tag="bank%d" % bank)
-            src = raws[n][:].rearrange("p (j c i) -> p c j i", j=PACK, i=4)
+            src = raws[n][:].rearrange("p (j c i) -> p j c i", j=PACK, i=4)
             if chunks[n][0] == "gate":
-                dst = pt[:].rearrange("p (i c j) -> p c j i", i=4, j=PACK)
+                dst = pt[:].rearrange("p (i c j) -> p j c i", i=4, j=PACK)
             else:
-                dst = pt[:].rearrange("p (c i j) -> p c j i", i=4, j=PACK)
+                dst = pt[:].rearrange("p (c i j) -> p j c i", i=4, j=PACK)
             c0 = (UNITS - T_COLS) // 4
             for h in range(2):
                 nc.tensor.matmul(
-                    out=dst[:, 32 * h:32 * h + 32], lhsT=ident_bf[:],
-                    rhs=src[:, c0 + 32 * h:c0 + 32 * h + 32], start=True, stop=True)
+                    out=dst[:, :, 32 * h:32 * h + 32], lhsT=ident_bf[:],
+                    rhs=src[:, :, c0 + 32 * h:c0 + 32 * h + 32], start=True, stop=True)
             pts[n] = pt
 
         def quant(n):
@@ -258,12 +258,6 @@ def tile_multidimensinalgrucell_pa_kernel(
         make_identity(nc, ident_bf[:])
         warm = const.tile([P, 2], F32, name="warm")
         nc.vector.memset(warm[:], 0.0)
-        for gi, b in enumerate((b_rl, b_rt, b_rd)):
-            bias = const.tile([P, 8], BF16, name="bias%d" % gi)
-            nc.gpsimd.dma_start(
-                out=bias[:].rearrange("p (g t) -> p g t", t=PACK),
-                in_=b.rearrange("(g p t) -> p g t", p=P, t=PACK))
-            biases[gi] = bias
         warm2 = const.tile([P, 2], F32, name="warm2")
         nc.scalar.activation(out=warm2[:, 0:1], in_=warm[:, 0:1], func=ACT.Sigmoid)
 
@@ -273,6 +267,12 @@ def tile_multidimensinalgrucell_pa_kernel(
             load_q(i)
         for n in range(5, RAW_BUFS):
             load(n)
+        for gi, b in enumerate((b_rl, b_rt, b_rd)):
+            bias = const.tile([P, 8], BF16, name="bias%d" % gi)
+            nc.sync.dma_start(
+                out=bias[:].rearrange("p (g t) -> p g t", t=PACK),
+                in_=b.rearrange("(g p t) -> p g t", p=P, t=PACK))
+            biases[gi] = bias
 
         bias_bc = const.tile([P, UNITS], BF16, name="bias_bc")
 

@@ -16,30 +16,49 @@ PACK = 4
 K_PASS = P * PACK
 BATCH = 256
 UNITS = 1024
+HALF = UNITS // 2
+N_CHUNKS = 32
+SPLIT = 32
+N_STEPS = SPLIT + 2 * (N_CHUNKS - SPLIT)
 FLOPS = 2 * BATCH * (4 * UNITS * 3 * UNITS + UNITS * UNITS + 3 * UNITS * UNITS)
 
 RAW_BUFS = 8
+EARLY = 9
 
 
-T_COLS = 256
+def part(n):
+    if n < SPLIT:
+        return n, 0, UNITS
+    left = N_CHUNKS - SPLIT
+    return SPLIT + (n - SPLIT) % left, HALF * ((n - SPLIT) // left), HALF
 
 
-def carried(n):
-    return n < 2 or (n >= 6 and n % 8 != 2)
+def t_cols(n):
+    if n < 10:
+        return 256 if n in (4, 6, 8) else 0
+    if n < SPLIT and n % 8 == 2:
+        return 0
+    return 256 * part(n)[2] // UNITS
+
+
+def pieces(n):
+    return {0: 4, 1: 2}.get(n, 1)
 
 
 def v_cols(n):
+    if n == 31:
+        return 320
     if n in (10, 18, 26):
-        return 800
+        return 864
     if n in (12, 20, 28):
         return 104
     if n in (13, 21, 29):
-        return 200
-    if n == 31:
-        return 384
-    if 2 <= n <= 5:
+        return 176
+    if not t_cols(n):
         return 560
-    return 416
+    if n in (3, 5, 7, 9):
+        return 480
+    return 408
 
 
 def tile_multidimensinalgrucell_pa_kernel(
@@ -55,41 +74,31 @@ def tile_multidimensinalgrucell_pa_kernel(
         chunks.append(("wi", w_i, c, 0))
     for c in range(6):
         chunks.append(("u", u, c, 0))
-    n_chunks = len(chunks)
     q_inputs = (left_state, top_state, diagonal_state, x)
 
     with ExitStack() as ctx:
         const = ctx.enter_context(tc.tile_pool(name="const", bufs=1))
         rawp = ctx.enter_context(tc.tile_pool(name="rawp", bufs=RAW_BUFS))
         grpp = ctx.enter_context(tc.tile_pool(name="grpp", bufs=4))
-        codep = ctx.enter_context(tc.tile_pool(name="codep", bufs=5))
+        codep = ctx.enter_context(tc.tile_pool(name="codep", bufs=6))
         sigp = ctx.enter_context(tc.tile_pool(name="sigp", bufs=2))
         outp = ctx.enter_context(tc.tile_pool(name="outp", bufs=4))
         psum = ctx.enter_context(tc.psum_pool(name="psum", bufs=1))
         ctx.enter_context(tc.manual_schedule())
 
-        raws = {}
-        grps = {}
-        codes = {}
-        scls = {}
-        q_raw = {}
-        qg = {}
-        q_cod = {}
-        q_scl = {}
-        rs_cod = {}
-        rs_scl = {}
-        acc = {}
-        sigs = {}
-        biases = {}
-        pts = {}
-        xts = {}
+        raws, grps, pts, codes, scls = {}, {}, {}, {}, {}
+        q_raw, xts, qg, q_cod, q_scl = {}, {}, {}, {}, {}
+        biases, acc, sigs, rs_cod, rs_scl = {}, {}, {}, {}, {}
 
-        def load(n):
-            w, c = chunks[n][1], chunks[n][2]
+        def load(m):
             raw = rawp.tile([P, PACK * UNITS], BF16, name="raw")
-            rows = w[c * K_PASS:(c + 1) * K_PASS, :]
-            nc.sync.dma_start(out=raw[:], in_=rows.rearrange("(p j) n -> p (j n)", j=PACK))
-            raws[n] = raw
+            rows = chunks[m][1][chunks[m][2] * K_PASS:(chunks[m][2] + 1) * K_PASS, :]
+            w = UNITS // pieces(m)
+            for c0 in range(0, UNITS, w):
+                nc.sync.dma_start(
+                    out=raw[:].rearrange("p (j n) -> p j n", j=PACK)[:, :, c0:c0 + w],
+                    in_=rows[:, c0:c0 + w].rearrange("(p j) n -> p j n", j=PACK))
+            raws[m] = raw
 
         def load_q(i):
             qr = const.tile([P, 2 * UNITS], BF16, name="q_raw%d" % i)
@@ -100,53 +109,65 @@ def tile_multidimensinalgrucell_pa_kernel(
             q_raw[i] = qr
 
         def regroup(n):
+            m, first, cols = part(n)
             grp = grpp.tile([P, PACK * UNITS], BF16, name="grp", align_bytes=64)
-            src = raws[n][:].rearrange("p (j c i) -> p c j i", j=PACK, i=4)
-            if chunks[n][0] == "gate":
+            src = raws[m][:].rearrange("p (j c i) -> p c j i", j=PACK, i=4)[
+                :, first // 4:(first + cols) // 4]
+            if chunks[m][0] == "gate":
                 dst = grp[:].rearrange("p (i c j) -> p c j i", i=4, j=PACK)
             else:
-                dst = grp[:].rearrange("p (c i j) -> p c j i", i=4, j=PACK)
-            cut = v_cols(n) // 4
-            end = (UNITS - T_COLS) // 4 if carried(n) else UNITS // 4
-            nc.vector.tensor_copy(out=dst[:, 0:cut], in_=src[:, 0:cut])
-            nc.scalar.copy(out=dst[:, cut:end], in_=src[:, cut:end])
-            if carried(n):
-                if chunks[n][0] == "gate":
+                dst = grp[:, 0:PACK * cols].rearrange("p (c i j) -> p c j i", i=4, j=PACK)
+            end = (cols - t_cols(n)) // 4
+            w = end // pieces(n)
+            v = v_cols(n) // 4 // pieces(n)
+            for c0 in range(0, end, w):
+                nc.vector.tensor_copy(out=dst[:, c0:c0 + v], in_=src[:, c0:c0 + v])
+                nc.scalar.copy(out=dst[:, c0 + v:c0 + w], in_=src[:, c0 + v:c0 + w])
+            if t_cols(n):
+                if chunks[m][0] == "gate":
                     laid = grp[:].rearrange("p (i c j) -> p i c j", i=4, j=PACK)[:, :, end:, :]
                     nc.scalar.copy(
                         out=laid.rearrange("p i c j -> p i (c j)"),
                         in_=pts[n][:].rearrange("p (i y) -> p i y", i=4))
                 else:
-                    nc.scalar.copy(out=grp[:, 4 * PACK * end:], in_=pts[n][:])
+                    nc.scalar.copy(out=grp[:, 4 * PACK * end:PACK * cols], in_=pts[n][:])
             grps[n] = grp
 
         def carry(n):
-            if n >= n_chunks or not carried(n):
+            if n >= N_STEPS or not t_cols(n):
                 return
+            m, first, cols = part(n)
             gi, r = n // 8, n % 8
-            bank = 4 * (gi % 2) + 2 + r if r < 2 else 4 * ((gi + 1) % 2) + r % 2
-            pt = psum.tile([P, PACK * T_COLS], BF16, name="pt%d" % n, tag="bank%d" % bank)
-            src = raws[n][:].rearrange("p (j c i) -> p j c i", j=PACK, i=4)
-            if chunks[n][0] == "gate":
+            if n < 10 or n >= 32:
+                bank = (6 if n < 10 else 0) + n % 2
+            elif r < 2:
+                bank = 4 * (gi % 2) + 2 + r
+            else:
+                bank = 4 * ((gi + 1) % 2) + r % 2
+            pt = psum.tile([P, PACK * t_cols(n)], BF16, name="pt%d" % n, tag="bank%d" % bank)
+            src = raws[m][:].rearrange("p (j c i) -> p j c i", j=PACK, i=4)
+            if chunks[m][0] == "gate":
                 dst = pt[:].rearrange("p (i c j) -> p j c i", i=4, j=PACK)
             else:
                 dst = pt[:].rearrange("p (c i j) -> p j c i", i=4, j=PACK)
-            c0 = (UNITS - T_COLS) // 4
-            for h in range(2):
+            c0 = (first + cols - t_cols(n)) // 4
+            w = t_cols(n) // 4 // 2
+            for h in range(0, 2 * w, w):
                 nc.tensor.matmul(
-                    out=dst[:, :, 32 * h:32 * h + 32], lhsT=ident_bf[:],
-                    rhs=src[:, :, c0 + 32 * h:c0 + 32 * h + 32], start=True, stop=True)
+                    out=dst[:, :, h:h + w], lhsT=ident_bf[:],
+                    rhs=src[:, :, c0 + h:c0 + h + w], start=True, stop=True)
             pts[n] = pt
 
         def quant(n):
+            cols = part(n)[2]
             cod = codep.tile([P, UNITS], U32, name="cod", align_bytes=64)
             scl = codep.tile([P, UNITS], U8, name="scl", align_bytes=64)
-            for half in range(2):
+            w = cols // 2 if n == N_STEPS - 1 else cols
+            for c0 in range(0, cols, w):
+                c1 = c0 + w
                 nc.vector.quantize_mx(
-                    out=cod[:, 512 * half:512 * half + 512].bitcast(FP8X4),
-                    scales=scl[:, 512 * half:512 * half + 512],
-                    in_=grps[n][:, 2048 * half:2048 * half + 2048],
-                )
+                    out=cod[:, c0:c1].bitcast(FP8X4), scales=scl[:, c0:c1],
+                    in_=grps[n][:, PACK * c0:PACK * c1])
             codes[n] = cod
             scls[n] = scl
 
@@ -154,14 +175,14 @@ def tile_multidimensinalgrucell_pa_kernel(
             for c in (2 * i, 2 * i + 1):
                 words = q_raw[i][:].bitcast(F32).rearrange(
                     "p (b h w e) -> p b h e w", b=2, h=2, w=P, e=2)
-                xt = psum.tile([P, 2, BATCH], F32, name="xt%d" % c, tag="bank%d" % (4 + c % 4))
+                xt = psum.tile([P, 2, BATCH], F32, name="xt%d" % c, tag="bank%d" % (4 + c % 2))
                 for e in range(2):
                     for b in range(2):
                         nc.tensor.transpose(
                             xt[:, e, b * P:(b + 1) * P], words[:, b, c % 2, e, :], ident[:])
                 xts[c] = xt
 
-        def q_finish(i):
+        def q_copy(i):
             for c in (2 * i, 2 * i + 1):
                 g = const.tile([P, PACK * BATCH], BF16, name="qg%d" % c, align_bytes=64)
                 nc.scalar.copy(
@@ -169,6 +190,8 @@ def tile_multidimensinalgrucell_pa_kernel(
                     in_=xts[c][:].rearrange("p e b -> p b e"),
                 )
                 qg[c] = g
+
+        def q_quant(i):
             for c in (2 * i, 2 * i + 1):
                 qc = const.tile([P, BATCH], U32, name="q_cod%d" % c, align_bytes=64)
                 qs = const.tile([P, BATCH], U8, name="q_scl%d" % c, align_bytes=64)
@@ -180,7 +203,8 @@ def tile_multidimensinalgrucell_pa_kernel(
             return 2 * P * (i % 4) + P * (i // 4)
 
         def mm(n):
-            kind, w, c, gi = chunks[n]
+            m, c_first, cols = part(n)
+            kind, w, c, gi = chunks[m]
             if kind == "gate":
                 for i in range(8):
                     if c == 0 and i % 2 == 0:
@@ -199,9 +223,9 @@ def tile_multidimensinalgrucell_pa_kernel(
             else:
                 first = kind == "wi" and c == 0
                 last = kind == "u" and c == 5
-                for h in range(2):
+                for c0 in range(0, cols, HALF):
                     for b in range(2):
-                        i = 2 * h + b
+                        i = 2 * ((c_first + c0) // HALF) + b
                         if first:
                             acc[i] = psum.tile([P, 512], F32, name="acc2_%d" % i, tag="bank%d" % (4 + i))
                         if kind == "wi":
@@ -212,8 +236,8 @@ def tile_multidimensinalgrucell_pa_kernel(
                             out=acc[i][:],
                             lhsT=a_cod[:, b * P:(b + 1) * P].bitcast(FP8X4),
                             lhsT_scale=a_scl[:, b * P:(b + 1) * P],
-                            rhs=codes[n][:, 512 * h:512 * h + 512].bitcast(FP8X4),
-                            rhs_scale=scls[n][:, 512 * h:512 * h + 512],
+                            rhs=codes[n][:, c0:c0 + HALF].bitcast(FP8X4),
+                            rhs_scale=scls[n][:, c0:c0 + HALF],
                             start=first,
                             stop=last,
                         )
@@ -252,6 +276,15 @@ def tile_multidimensinalgrucell_pa_kernel(
                 rs_cod[cc] = rc
                 rs_scl[cc] = rsc
 
+        def finish(h):
+            for b in range(2):
+                pre = outp.tile([P, 512], F32, name="pre")
+                nc.vector.tensor_tensor(
+                    out=pre[:], in0=acc[2 * h + b][:], in1=bias_bc[:, 512 * h:512 * h + 512], op=ALU.add)
+                res = outp.tile([P, 512], F32, name="res")
+                nc.scalar.activation(out=res[:], in_=pre[:], func=ACT.Tanh)
+                nc.sync.dma_start(out=out[b * P:(b + 1) * P, 512 * h:512 * h + 512], in_=res[:])
+
         ident = const.tile([P, P], F32, name="ident")
         make_identity(nc, ident[:])
         ident_bf = const.tile([P, P], BF16, name="ident_bf")
@@ -261,50 +294,48 @@ def tile_multidimensinalgrucell_pa_kernel(
         warm2 = const.tile([P, 2], F32, name="warm2")
         nc.scalar.activation(out=warm2[:, 0:1], in_=warm[:, 0:1], func=ACT.Sigmoid)
 
-        load(0)
-        for i in range(4):
-            load(i + 1)
-            load_q(i)
-        for n in range(5, RAW_BUFS):
-            load(n)
+        for m in range(RAW_BUFS):
+            load(m)
+            if m in (2, 4, 6):
+                load_q(m // 2 - 1)
         for gi, b in enumerate((b_rl, b_rt, b_rd)):
             bias = const.tile([P, 8], BF16, name="bias%d" % gi)
             nc.sync.dma_start(
                 out=bias[:].rearrange("p (g t) -> p g t", t=PACK),
                 in_=b.rearrange("(g p t) -> p g t", p=P, t=PACK))
             biases[gi] = bias
-
         bias_bc = const.tile([P, UNITS], BF16, name="bias_bc")
 
-        carry(0)
-        for n in range(n_chunks + 1):
-            if n < n_chunks:
+        for n in range(N_STEPS + 1):
+            if 1 <= n <= EARLY:
+                quant(n - 1)
+            if n in (3, 5, 7, 9):
+                q_quant(n // 2 - 1)
+            if n in (2, 4, 6, 8):
+                q_transposes(n // 2 - 1)
+            if n < N_STEPS:
                 regroup(n)
+            if n in (2, 4, 6, 8):
+                q_copy(n // 2 - 1)
             if n in (10, 18, 26):
                 sigmoids((n - 10) // 8)
-            if 1 <= n <= 4:
-                q_transposes(n - 1)
-            if n + RAW_BUFS < n_chunks:
+            if n + RAW_BUFS < N_CHUNKS:
                 load(n + RAW_BUFS)
+            if n == 0:
+                load_q(3)
             if n == 24:
                 nc.sync.dma_start(out=bias_bc[:], in_=b_i.partition_broadcast(P))
-            if n >= 1:
+            if n > EARLY:
                 quant(n - 1)
-            if 2 <= n <= 5:
-                q_finish(n - 2)
-            if n >= 2:
-                mm(n - 2)
+            for k in {9: (6, 7)}.get(n, (n - 3,) if n < 9 else (n - 2,)):
+                if k >= 0:
+                    mm(k)
             carry(n + 1)
             if n in (12, 20, 28):
                 products((n - 12) // 8)
-        mm(n_chunks - 1)
-
-        for h in range(2):
-            for b in range(2):
-                i = 2 * h + b
-                pre = outp.tile([P, 512], F32, name="pre")
-                nc.vector.tensor_tensor(
-                    out=pre[:], in0=acc[i][:], in1=bias_bc[:, 512 * h:512 * h + 512], op=ALU.add)
-                res = outp.tile([P, 512], F32, name="res")
-                nc.scalar.activation(out=res[:], in_=pre[:], func=ACT.Tanh)
-                nc.sync.dma_start(out=out[b * P:(b + 1) * P, 512 * h:512 * h + 512], in_=res[:])
+            if n == N_STEPS - 1 and SPLIT < N_CHUNKS:
+                finish(0)
+        mm(N_STEPS - 1)
+        if SPLIT == N_CHUNKS:
+            finish(0)
+        finish(1)

@@ -18,12 +18,12 @@ BATCH = 256
 UNITS = 1024
 HALF = UNITS // 2
 N_CHUNKS = 32
-SPLIT = 32
+SPLIT = 31
 N_STEPS = SPLIT + 2 * (N_CHUNKS - SPLIT)
 FLOPS = 2 * BATCH * (4 * UNITS * 3 * UNITS + UNITS * UNITS + 3 * UNITS * UNITS)
 
 RAW_BUFS = 8
-EARLY = 9
+EARLY = 4
 
 
 def part(n):
@@ -41,13 +41,9 @@ def t_cols(n):
     return 256 * part(n)[2] // UNITS
 
 
-def pieces(n):
-    return {0: 4, 1: 2}.get(n, 1)
-
-
 def v_cols(n):
-    if n == 31:
-        return 320
+    if n >= SPLIT:
+        return 160 if n == N_STEPS - 1 else 208
     if n in (10, 18, 26):
         return 864
     if n in (12, 20, 28):
@@ -93,11 +89,7 @@ def tile_multidimensinalgrucell_pa_kernel(
         def load(m):
             raw = rawp.tile([P, PACK * UNITS], BF16, name="raw")
             rows = chunks[m][1][chunks[m][2] * K_PASS:(chunks[m][2] + 1) * K_PASS, :]
-            w = UNITS // pieces(m)
-            for c0 in range(0, UNITS, w):
-                nc.sync.dma_start(
-                    out=raw[:].rearrange("p (j n) -> p j n", j=PACK)[:, :, c0:c0 + w],
-                    in_=rows[:, c0:c0 + w].rearrange("(p j) n -> p j n", j=PACK))
+            nc.sync.dma_start(out=raw[:], in_=rows.rearrange("(p j) n -> p (j n)", j=PACK))
             raws[m] = raw
 
         def load_q(i):
@@ -118,11 +110,9 @@ def tile_multidimensinalgrucell_pa_kernel(
             else:
                 dst = grp[:, 0:PACK * cols].rearrange("p (c i j) -> p c j i", i=4, j=PACK)
             end = (cols - t_cols(n)) // 4
-            w = end // pieces(n)
-            v = v_cols(n) // 4 // pieces(n)
-            for c0 in range(0, end, w):
-                nc.vector.tensor_copy(out=dst[:, c0:c0 + v], in_=src[:, c0:c0 + v])
-                nc.scalar.copy(out=dst[:, c0 + v:c0 + w], in_=src[:, c0 + v:c0 + w])
+            v = v_cols(n) // 4
+            nc.vector.tensor_copy(out=dst[:, 0:v], in_=src[:, 0:v])
+            nc.scalar.copy(out=dst[:, v:end], in_=src[:, v:end])
             if t_cols(n):
                 if chunks[m][0] == "gate":
                     laid = grp[:].rearrange("p (i c j) -> p i c j", i=4, j=PACK)[:, :, end:, :]
@@ -162,9 +152,8 @@ def tile_multidimensinalgrucell_pa_kernel(
             cols = part(n)[2]
             cod = codep.tile([P, UNITS], U32, name="cod", align_bytes=64)
             scl = codep.tile([P, UNITS], U8, name="scl", align_bytes=64)
-            w = cols // 2 if n == N_STEPS - 1 else cols
-            for c0 in range(0, cols, w):
-                c1 = c0 + w
+            for c0 in range(0, cols, 1024):
+                c1 = min(c0 + 1024, cols)
                 nc.vector.quantize_mx(
                     out=cod[:, c0:c1].bitcast(FP8X4), scales=scl[:, c0:c1],
                     in_=grps[n][:, PACK * c0:PACK * c1])
@@ -333,9 +322,6 @@ def tile_multidimensinalgrucell_pa_kernel(
             carry(n + 1)
             if n in (12, 20, 28):
                 products((n - 12) // 8)
-            if n == N_STEPS - 1 and SPLIT < N_CHUNKS:
-                finish(0)
+        finish(0)
         mm(N_STEPS - 1)
-        if SPLIT == N_CHUNKS:
-            finish(0)
         finish(1)

@@ -23,7 +23,7 @@ N_STEPS = SPLIT + 2 * (N_CHUNKS - SPLIT)
 FLOPS = 2 * BATCH * (4 * UNITS * 3 * UNITS + UNITS * UNITS + 3 * UNITS * UNITS)
 
 RAW_BUFS = 8
-EARLY = 4
+EARLY = 9
 
 
 def part(n):
@@ -35,7 +35,7 @@ def part(n):
 
 def t_cols(n):
     if n < 10:
-        return 256 if n in (4, 6, 8) else 0
+        return 256 if n in (4, 6, 7, 8, 9) else 0
     if n < SPLIT and n % 8 == 2:
         return 0
     return 256 * part(n)[2] // UNITS
@@ -54,7 +54,7 @@ def v_cols(n):
         return 560
     if n in (3, 5, 7, 9):
         return 480
-    return 408
+    return 424
 
 
 def tile_multidimensinalgrucell_pa_kernel(
@@ -84,7 +84,7 @@ def tile_multidimensinalgrucell_pa_kernel(
 
         raws, grps, pts, codes, scls = {}, {}, {}, {}, {}
         q_raw, xts, qg, q_cod, q_scl = {}, {}, {}, {}, {}
-        biases, acc, sigs, rs_cod, rs_scl = {}, {}, {}, {}, {}
+        acc, sigs, rs_cod, rs_scl = {}, {}, {}, {}
 
         def load(m):
             raw = rawp.tile([P, PACK * UNITS], BF16, name="raw")
@@ -95,9 +95,7 @@ def tile_multidimensinalgrucell_pa_kernel(
         def load_q(i):
             qr = const.tile([P, 2 * UNITS], BF16, name="q_raw%d" % i)
             nc.sync.dma_start(
-                out=qr[:].rearrange("p (b k) -> p b k", b=2),
-                in_=q_inputs[i].rearrange("(b p) k -> p b k", p=P),
-            )
+                out=qr[:], in_=q_inputs[i].rearrange("(p b) k -> p (b k)", b=2))
             q_raw[i] = qr
 
         def regroup(n):
@@ -240,7 +238,7 @@ def tile_multidimensinalgrucell_pa_kernel(
                         out=sig[:, t * BATCH:(t + 1) * BATCH],
                         in_=acc[i // 2][:, (i % 2) * BATCH:(i % 2 + 1) * BATCH],
                         func=ACT.Sigmoid,
-                        bias=biases[gi][:, i:i + 1],
+                        bias=bias_f[:, t, 2 * gi + g:2 * gi + g + 1],
                         scale=1.0,
                     )
                 sigs[g] = sig
@@ -272,7 +270,9 @@ def tile_multidimensinalgrucell_pa_kernel(
                     out=pre[:], in0=acc[2 * h + b][:], in1=bias_bc[:, 512 * h:512 * h + 512], op=ALU.add)
                 res = outp.tile([P, 512], F32, name="res")
                 nc.scalar.activation(out=res[:], in_=pre[:], func=ACT.Tanh)
-                nc.sync.dma_start(out=out[b * P:(b + 1) * P, 512 * h:512 * h + 512], in_=res[:])
+                nc.sync.dma_start(
+                    out=out.rearrange("(p b) n -> b p n", b=2)[b, :, HALF * h:HALF * h + HALF],
+                    in_=res[:])
 
         ident = const.tile([P, P], F32, name="ident")
         make_identity(nc, ident[:])
@@ -283,17 +283,36 @@ def tile_multidimensinalgrucell_pa_kernel(
         warm2 = const.tile([P, 2], F32, name="warm2")
         nc.scalar.activation(out=warm2[:, 0:1], in_=warm[:, 0:1], func=ACT.Sigmoid)
 
+        gate_rows = const.tile([P, 512], BF16, name="gate_rows")
+        nc.vector.memset(gate_rows[:], 0.0)
+        bi_row = const.tile([P, UNITS], BF16, name="bi_row")
+        nc.vector.memset(bi_row[:], 0.0)
+        for gi, b in enumerate((b_rl, b_rt, b_rd)):
+            nc.gpsimd.dma_start(
+                out=gate_rows[2 * gi:2 * gi + 2, :], in_=b.rearrange("(g m) -> g m", g=2))
+        nc.gpsimd.dma_start(out=bi_row[0:1, :], in_=b_i.rearrange("(a n) -> a n", a=1))
+        ones = const.tile([P, P], BF16, name="ones")
+        nc.vector.memset(ones[:], 1.0)
         for m in range(RAW_BUFS):
             load(m)
             if m in (2, 4, 6):
                 load_q(m // 2 - 1)
-        for gi, b in enumerate((b_rl, b_rt, b_rd)):
-            bias = const.tile([P, 8], BF16, name="bias%d" % gi)
-            nc.sync.dma_start(
-                out=bias[:].rearrange("p (g t) -> p g t", t=PACK),
-                in_=b.rearrange("(g p t) -> p g t", p=P, t=PACK))
-            biases[gi] = bias
+
+        bias_f = const.tile([P, PACK, 6], F32, name="bias_f")
         bias_bc = const.tile([P, UNITS], BF16, name="bias_bc")
+
+        def lay_biases():
+            bt = psum.tile([P, PACK, P], BF16, name="bt", tag="bank6")
+            for t in range(PACK):
+                nc.tensor.transpose(
+                    bt[:, t, :], gate_rows[:].rearrange("p (m t) -> p t m", t=PACK)[:, t, :], ident_bf[:])
+            nc.vector.tensor_copy(out=bias_f[:], in_=bt[:, :, 0:6])
+            bb = psum.tile([P, UNITS], BF16, name="bb", tag="bank7")
+            for h in range(2):
+                nc.tensor.matmul(
+                    out=bb[:, HALF * h:HALF * h + HALF], lhsT=ones[:],
+                    rhs=bi_row[:, HALF * h:HALF * h + HALF], start=True, stop=True)
+            nc.scalar.copy(out=bias_bc[:], in_=bb[:])
 
         for n in range(N_STEPS + 1):
             if 1 <= n <= EARLY:
@@ -312,8 +331,8 @@ def tile_multidimensinalgrucell_pa_kernel(
                 load(n + RAW_BUFS)
             if n == 0:
                 load_q(3)
-            if n == 24:
-                nc.sync.dma_start(out=bias_bc[:], in_=b_i.partition_broadcast(P))
+            if n == 1:
+                lay_biases()
             if n > EARLY:
                 quant(n - 1)
             for k in {9: (6, 7)}.get(n, (n - 3,) if n < 9 else (n - 2,)):

@@ -287,14 +287,15 @@ def tile_multidimensinalgrucell_pa_kernel(
         nc.vector.memset(gate_rows[:], 0.0)
         bi_row = const.tile([P, UNITS], BF16, name="bi_row")
         nc.vector.memset(bi_row[:], 0.0)
-        for gi, b in enumerate((b_rl, b_rt, b_rd)):
-            nc.gpsimd.dma_start(
-                out=gate_rows[2 * gi:2 * gi + 2, :], in_=b.rearrange("(g m) -> g m", g=2))
-        nc.gpsimd.dma_start(out=bi_row[0:1, :], in_=b_i.rearrange("(a n) -> a n", a=1))
         ones = const.tile([P, P], BF16, name="ones")
         nc.vector.memset(ones[:], 1.0)
         for m in range(RAW_BUFS):
             load(m)
+            if m == 1:
+                for gi, b in enumerate((b_rl, b_rt, b_rd)):
+                    nc.sync.dma_start(
+                        out=gate_rows[2 * gi:2 * gi + 2, :], in_=b.rearrange("(g m) -> g m", g=2))
+                nc.sync.dma_start(out=bi_row[0:1, :], in_=b_i.rearrange("(a n) -> a n", a=1))
             if m in (2, 4, 6):
                 load_q(m // 2 - 1)
 
@@ -331,7 +332,7 @@ def tile_multidimensinalgrucell_pa_kernel(
                 load(n + RAW_BUFS)
             if n == 0:
                 load_q(3)
-            if n == 1:
+            if n == 2:
                 lay_biases()
             if n > EARLY:
                 quant(n - 1)

from contextlib import ExitStack

import concourse.mybir as mybir
from concourse.masks import make_identity

F32 = mybir.dt.float32
BF16 = mybir.dt.bfloat16
U32 = mybir.dt.uint32
U8 = mybir.dt.uint8
FP8X4 = mybir.dt.float8_e4m3fn_x4
ACT = mybir.ActivationFunctionType
ALU = mybir.AluOpType

P = 128
PACK = 4
K_PASS = P * PACK
BATCH = 256
UNITS = 1024
HALF = UNITS // 2
N_CHUNKS = 32
SPLIT = 31
N_STEPS = SPLIT + 2 * (N_CHUNKS - SPLIT)
FLOPS = 2 * BATCH * (4 * UNITS * 3 * UNITS + UNITS * UNITS + 3 * UNITS * UNITS)

RAW_BUFS = 8
EARLY = 9


def part(n):
    if n < SPLIT:
        return n, 0, UNITS
    left = N_CHUNKS - SPLIT
    return SPLIT + (n - SPLIT) % left, HALF * ((n - SPLIT) // left), HALF


def t_cols(n):
    if n < 10:
        return 256 if n in (4, 6, 7, 8, 9) else 0
    if n < SPLIT and n % 8 == 2:
        return 0
    return 256 * part(n)[2] // UNITS


def v_cols(n):
    if n >= SPLIT:
        return 160 if n == N_STEPS - 1 else 208
    if n in (10, 18, 26):
        return 864
    if n in (12, 20, 28):
        return 104
    if n in (13, 21, 29):
        return 176
    if not t_cols(n):
        return 560
    if n in (3, 5, 7, 9):
        return 480
    return 424


def tile_multidimensinalgrucell_pa_kernel(
    tc, x, left_state, top_state, diagonal_state,
    w_rl, b_rl, w_rt, b_rt, w_rd, b_rd, u, w_i, b_i, out,
):
    nc = tc.nc
    chunks = []
    for gi, w in enumerate((w_rl, w_rt, w_rd)):
        for c in range(8):
            chunks.append(("gate", w, c, gi))
    for c in range(2):
        chunks.append(("wi", w_i, c, 0))
    for c in range(6):
        chunks.append(("u", u, c, 0))
    q_inputs = (left_state, top_state, diagonal_state, x)

    with ExitStack() as ctx:
        const = ctx.enter_context(tc.tile_pool(name="const", bufs=1))
        rawp = ctx.enter_context(tc.tile_pool(name="rawp", bufs=RAW_BUFS))
        grpp = ctx.enter_context(tc.tile_pool(name="grpp", bufs=4))
        codep = ctx.enter_context(tc.tile_pool(name="codep", bufs=6))
        sigp = ctx.enter_context(tc.tile_pool(name="sigp", bufs=2))
        outp = ctx.enter_context(tc.tile_pool(name="outp", bufs=4))
        psum = ctx.enter_context(tc.psum_pool(name="psum", bufs=1))
        ctx.enter_context(tc.manual_schedule())

        raws, grps, pts, codes, scls = {}, {}, {}, {}, {}
        q_raw, xts, qg, q_cod, q_scl = {}, {}, {}, {}, {}
        acc, sigs, rs_cod, rs_scl = {}, {}, {}, {}

        def load(m):
            raw = rawp.tile([P, PACK * UNITS], BF16, name="raw")
            rows = chunks[m][1][chunks[m][2] * K_PASS:(chunks[m][2] + 1) * K_PASS, :]
            nc.sync.dma_start(out=raw[:], in_=rows.rearrange("(p j) n -> p (j n)", j=PACK))
            raws[m] = raw

        def load_q(i):
            qr = const.tile([P, 2 * UNITS], BF16, name="q_raw%d" % i)
            nc.sync.dma_start(
                out=qr[:], in_=q_inputs[i].rearrange("(p b) k -> p (b k)", b=2))
            q_raw[i] = qr

        def regroup(n):
            m, first, cols = part(n)
            grp = grpp.tile([P, PACK * UNITS], BF16, name="grp", align_bytes=64)
            src = raws[m][:].rearrange("p (j c i) -> p c j i", j=PACK, i=4)[
                :, first // 4:(first + cols) // 4]
            if chunks[m][0] == "gate":
                dst = grp[:].rearrange("p (i c j) -> p c j i", i=4, j=PACK)
            else:
                dst = grp[:, 0:PACK * cols].rearrange("p (c i j) -> p c j i", i=4, j=PACK)
            end = (cols - t_cols(n)) // 4
            v = v_cols(n) // 4
            nc.vector.tensor_copy(out=dst[:, 0:v], in_=src[:, 0:v])
            nc.scalar.copy(out=dst[:, v:end], in_=src[:, v:end])
            if t_cols(n):
                if chunks[m][0] == "gate":
                    laid = grp[:].rearrange("p (i c j) -> p i c j", i=4, j=PACK)[:, :, end:, :]
                    nc.scalar.copy(
                        out=laid.rearrange("p i c j -> p i (c j)"),
                        in_=pts[n][:].rearrange("p (i y) -> p i y", i=4))
                else:
                    nc.scalar.copy(out=grp[:, 4 * PACK * end:PACK * cols], in_=pts[n][:])
            grps[n] = grp

        def carry(n):
            if n >= N_STEPS or not t_cols(n):
                return
            m, first, cols = part(n)
            gi, r = n // 8, n % 8
            if n < 10 or n >= 32:
                bank = (6 if n < 10 else 0) + n % 2
            elif r < 2:
                bank = 4 * (gi % 2) + 2 + r
            else:
                bank = 4 * ((gi + 1) % 2) + r % 2
            pt = psum.tile([P, PACK * t_cols(n)], BF16, name="pt%d" % n, tag="bank%d" % bank)
            src = raws[m][:].rearrange("p (j c i) -> p j c i", j=PACK, i=4)
            if chunks[m][0] == "gate":
                dst = pt[:].rearrange("p (i c j) -> p j c i", i=4, j=PACK)
            else:
                dst = pt[:].rearrange("p (c i j) -> p j c i", i=4, j=PACK)
            c0 = (first + cols - t_cols(n)) // 4
            w = t_cols(n) // 4 // 2
            for h in range(0, 2 * w, w):
                nc.tensor.matmul(
                    out=dst[:, :, h:h + w], lhsT=ident_bf[:],
                    rhs=src[:, :, c0 + h:c0 + h + w], start=True, stop=True)
            pts[n] = pt

        def quant(n):
            cols = part(n)[2]
            cod = codep.tile([P, UNITS], U32, name="cod", align_bytes=64)
            scl = codep.tile([P, UNITS], U8, name="scl", align_bytes=64)
            for c0 in range(0, cols, 1024):
                c1 = min(c0 + 1024, cols)
                nc.vector.quantize_mx(
                    out=cod[:, c0:c1].bitcast(FP8X4), scales=scl[:, c0:c1],
                    in_=grps[n][:, PACK * c0:PACK * c1])
            codes[n] = cod
            scls[n] = scl

        def q_transposes(i):
            for c in (2 * i, 2 * i + 1):
                words = q_raw[i][:].bitcast(F32).rearrange(
                    "p (b h w e) -> p b h e w", b=2, h=2, w=P, e=2)
                xt = psum.tile([P, 2, BATCH], F32, name="xt%d" % c, tag="bank%d" % (4 + c % 2))
                for e in range(2):
                    for b in range(2):
                        nc.tensor.transpose(
                            xt[:, e, b * P:(b + 1) * P], words[:, b, c % 2, e, :], ident[:])
                xts[c] = xt

        def q_copy(i):
            for c in (2 * i, 2 * i + 1):
                g = const.tile([P, PACK * BATCH], BF16, name="qg%d" % c, align_bytes=64)
                nc.scalar.copy(
                    out=g[:].bitcast(F32).rearrange("p (b e) -> p b e", e=2),
                    in_=xts[c][:].rearrange("p e b -> p b e"),
                )
                qg[c] = g

        def q_quant(i):
            for c in (2 * i, 2 * i + 1):
                qc = const.tile([P, BATCH], U32, name="q_cod%d" % c, align_bytes=64)
                qs = const.tile([P, BATCH], U8, name="q_scl%d" % c, align_bytes=64)
                nc.vector.quantize_mx(out=qc[:].bitcast(FP8X4), scales=qs[:], in_=qg[c][:])
                q_cod[c] = qc
                q_scl[c] = qs

        def tile0(i):
            return 2 * P * (i % 4) + P * (i // 4)

        def mm(n):
            m, c_first, cols = part(n)
            kind, w, c, gi = chunks[m]
            if kind == "gate":
                for i in range(8):
                    if c == 0 and i % 2 == 0:
                        acc[i // 2] = psum.tile(
                            [P, 512], F32, name="acc%d_%d" % (gi, i // 2),
                            tag="bank%d" % (4 * (gi % 2) + i // 2))
                    nc.tensor.matmul_mx(
                        out=acc[i // 2][:, (i % 2) * BATCH:(i % 2 + 1) * BATCH],
                        lhsT=codes[n][:, tile0(i):tile0(i) + P].bitcast(FP8X4),
                        lhsT_scale=scls[n][:, tile0(i):tile0(i) + P],
                        rhs=q_cod[c][:].bitcast(FP8X4),
                        rhs_scale=q_scl[c][:],
                        start=(c == 0 and i % 2 == 0),
                        stop=(c == 7 and i % 2 == 1),
                    )
            else:
                first = kind == "wi" and c == 0
                last = kind == "u" and c == 5
                for c0 in range(0, cols, HALF):
                    for b in range(2):
                        i = 2 * ((c_first + c0) // HALF) + b
                        if first:
                            acc[i] = psum.tile([P, 512], F32, name="acc2_%d" % i, tag="bank%d" % (4 + i))
                        if kind == "wi":
                            a_cod, a_scl = q_cod[6 + c], q_scl[6 + c]
                        else:
                            a_cod, a_scl = rs_cod[c], rs_scl[c]
                        nc.tensor.matmul_mx(
                            out=acc[i][:],
                            lhsT=a_cod[:, b * P:(b + 1) * P].bitcast(FP8X4),
                            lhsT_scale=a_scl[:, b * P:(b + 1) * P],
                            rhs=codes[n][:, c0:c0 + HALF].bitcast(FP8X4),
                            rhs_scale=scls[n][:, c0:c0 + HALF],
                            start=first,
                            stop=last,
                        )

        def sigmoids(gi):
            for g in range(2):
                sig = sigp.tile([P, PACK * BATCH], F32, name="sig")
                for t in range(PACK):
                    i = 4 * g + t
                    nc.scalar.activation(
                        out=sig[:, t * BATCH:(t + 1) * BATCH],
                        in_=acc[i // 2][:, (i % 2) * BATCH:(i % 2 + 1) * BATCH],
                        func=ACT.Sigmoid,
                        bias=bias_f[:, t, 2 * gi + g:2 * gi + g + 1],
                        scale=1.0,
                    )
                sigs[g] = sig
            if gi == 2:
                nc.scalar.activation(out=warm2[:, 1:2], in_=sigs[1][:, 0:1], func=ACT.Tanh)

        def products(gi):
            for g in range(2):
                rsg = sigp.tile([P, PACK * BATCH], BF16, name="rsg", align_bytes=64)
                nc.vector.tensor_tensor(
                    out=rsg[:].rearrange("p (b t) -> p b t", t=PACK),
                    in0=sigs[g][:].rearrange("p (t b) -> p b t", t=PACK),
                    in1=qg[2 * gi + g][:].rearrange("p (b t) -> p b t", t=PACK),
                    op=ALU.mult,
                )
                sigs[2 + g] = rsg
            for g in range(2):
                cc = 2 * gi + g
                rc = const.tile([P, BATCH], U32, name="rs_cod%d" % cc, align_bytes=64)
                rsc = const.tile([P, BATCH], U8, name="rs_scl%d" % cc, align_bytes=64)
                nc.vector.quantize_mx(out=rc[:].bitcast(FP8X4), scales=rsc[:], in_=sigs[2 + g][:])
                rs_cod[cc] = rc
                rs_scl[cc] = rsc

        def finish(h):
            for b in range(2):
                pre = outp.tile([P, 512], F32, name="pre")
                nc.vector.tensor_tensor(
                    out=pre[:], in0=acc[2 * h + b][:], in1=bias_bc[:, 512 * h:512 * h + 512], op=ALU.add)
                res = outp.tile([P, 512], F32, name="res")
                nc.scalar.activation(out=res[:], in_=pre[:], func=ACT.Tanh)
                nc.sync.dma_start(
                    out=out.rearrange("(p b) n -> b p n", b=2)[b, :, HALF * h:HALF * h + HALF],
                    in_=res[:])

        ident = const.tile([P, P], F32, name="ident")
        make_identity(nc, ident[:])
        ident_bf = const.tile([P, P], BF16, name="ident_bf")
        make_identity(nc, ident_bf[:])
        warm = const.tile([P, 2], F32, name="warm")
        nc.vector.memset(warm[:], 0.0)
        warm2 = const.tile([P, 2], F32, name="warm2")
        nc.scalar.activation(out=warm2[:, 0:1], in_=warm[:, 0:1], func=ACT.Sigmoid)

        gate_rows = const.tile([P, 512], BF16, name="gate_rows")
        nc.vector.memset(gate_rows[:], 0.0)
        bi_row = const.tile([P, UNITS], BF16, name="bi_row")
        nc.vector.memset(bi_row[:], 0.0)
        ones = const.tile([P, P], BF16, name="ones")
        nc.vector.memset(ones[:], 1.0)
        for m in range(RAW_BUFS):
            load(m)
            if m == 1:
                for gi, b in enumerate((b_rl, b_rt, b_rd)):
                    nc.sync.dma_start(
                        out=gate_rows[2 * gi:2 * gi + 2, :], in_=b.rearrange("(g m) -> g m", g=2))
                nc.sync.dma_start(out=bi_row[0:1, :], in_=b_i.rearrange("(a n) -> a n", a=1))
            if m in (2, 4, 6):
                load_q(m // 2 - 1)

        bias_f = const.tile([P, PACK, 6], F32, name="bias_f")
        bias_bc = const.tile([P, UNITS], BF16, name="bias_bc")

        def lay_biases():
            bt = psum.tile([P, PACK, P], BF16, name="bt", tag="bank6")
            for t in range(PACK):
                nc.tensor.transpose(
                    bt[:, t, :], gate_rows[:].rearrange("p (m t) -> p t m", t=PACK)[:, t, :], ident_bf[:])
            nc.vector.tensor_copy(out=bias_f[:], in_=bt[:, :, 0:6])
            bb = psum.tile([P, UNITS], BF16, name="bb", tag="bank7")
            for h in range(2):
                nc.tensor.matmul(
                    out=bb[:, HALF * h:HALF * h + HALF], lhsT=ones[:],
                    rhs=bi_row[:, HALF * h:HALF * h + HALF], start=True, stop=True)
            nc.scalar.copy(out=bias_bc[:], in_=bb[:])

        for n in range(N_STEPS + 1):
            if 1 <= n <= EARLY:
                quant(n - 1)
            if n in (3, 5, 7, 9):
                q_quant(n // 2 - 1)
            if n in (2, 4, 6, 8):
                q_transposes(n // 2 - 1)
            if n < N_STEPS:
                regroup(n)
            if n in (2, 4, 6, 8):
                q_copy(n // 2 - 1)
            if n in (10, 18, 26):
                sigmoids((n - 10) // 8)
            if n + RAW_BUFS < N_CHUNKS:
                load(n + RAW_BUFS)
            if n == 0:
                load_q(3)
            if n == 2:
                lay_biases()
            if n > EARLY:
                quant(n - 1)
            for k in {9: (6, 7)}.get(n, (n - 3,) if n < 9 else (n - 2,)):
                if k >= 0:
                    mm(k)
            carry(n + 1)
            if n in (12, 20, 28):
                products((n - 12) // 8)
        finish(0)
        mm(N_STEPS - 1)
        finish(1)
